import numpy as np
import ml_dtypes


def mxq(x, axis, fmt="e4m3"):
    dtype, down = {"e4m3": (ml_dtypes.float8_e4m3fn, 7), "e5m2": (ml_dtypes.float8_e5m2, 14)}[fmt]
    v = np.moveaxis(np.asarray(x, np.float32).astype(ml_dtypes.bfloat16).astype(np.float64), axis, -1)
    blocks = v.reshape(v.shape[:-1] + (-1, 32))
    amax = np.abs(blocks).max(-1, keepdims=True)
    byte = np.maximum(np.where(amax > 0, np.frexp(amax)[1] - 1 + 127, 0) - down, 1)
    scale = np.exp2(byte - 127.0)
    codes = (blocks / scale).astype(np.float32).astype(dtype).astype(np.float64)
    return np.moveaxis((codes * scale).reshape(v.shape), -1, axis)


WIDE = False


def mx_kscale(k):
    if not WIDE:
        return np.ones(k)
    levels = np.array([10, -10, 5, -5, 0])
    a = np.random.permutation(np.resize(levels, k // 512 * 4)).reshape(k // 512, 4)
    idx = np.arange(k)
    return np.exp2(a[idx // 512, idx % 128 // 32])


BF16 = ml_dtypes.bfloat16


def bf(x):
    return np.asarray(x, np.float32).astype(BF16)


def f64(x):
    return np.asarray(x).astype(np.float64)


B, N, F = 4, 1024, 512


def setup_inputs():
    s = mx_kscale(F)
    limit = np.sqrt(6.0 / (F + F))
    return {"nodes": bf(np.random.standard_normal((B, N, F)) * s),
            "W": bf(np.random.uniform(-limit, limit, (F, F)) / s[:, None] / s[None, :])}


def reference(nodes, W):
    norm_const = 1.0 / np.sqrt(F)
    nq = mxq(f64(nodes), 2, "e4m3")
    x = nq @ mxq(f64(W), 0, "e4m3")
    prods = mxq(x, 2, "e4m3") @ nq.transpose(0, 2, 1)
    z = prods * norm_const
    e = np.exp(z - z.max(-1, keepdims=True))
    return e / e.sum(-1, keepdims=True)

@@ -1,0 +1,295 @@
+from contextlib import ExitStack
+import math
+
+import concourse.mybir as mybir
+from concourse.masks import make_identity
+
+F32 = mybir.dt.float32
+BF16 = mybir.dt.bfloat16
+U32 = mybir.dt.uint32
+U8 = mybir.dt.uint8
+FP8X4 = mybir.dt.float8_e4m3fn_x4
+ALU = mybir.AluOpType
+ACT = mybir.ActivationFunctionType
+AX = mybir.AxisListType
+
+B, N, F = 4, 1024, 512
+P = 128
+RT = N // P
+NT = B * RT
+NORM = 1.0 / math.sqrt(F)
+FLOPS = 2 * B * (N * F * F + N * N * F)
+
+
+def tile_scalarproductattentiont_pa_t_kernel(tc, nodes, W, out):
+    nc = tc.nc
+    with ExitStack() as ctx:
+        keep = ctx.enter_context(tc.tile_pool(name="keep", bufs=1))
+        grp = ctx.enter_context(tc.tile_pool(name="grp", bufs=2))
+        epool = ctx.enter_context(tc.tile_pool(name="epool", bufs=10))
+        small = ctx.enter_context(tc.tile_pool(name="small", bufs=8))
+        ps_pr = ctx.enter_context(tc.psum_pool(name="ps_pr", bufs=3))
+        ps_aux = ctx.enter_context(tc.psum_pool(name="ps_aux", bufs=2))
+
+        ident = keep.tile([P, P], F32, name="ident")
+        make_identity(nc, ident[:])
+
+        warm = keep.tile([P, 1], F32, name="warm")
+        nc.vector.memset(warm[:], 0.0)
+        nc.scalar.activation(out=warm[:], in_=warm[:], func=ACT.Exp)
+
+        w_raw = keep.tile([P, 4, F], BF16, name="w_raw")
+        nc.sync.dma_start(
+            out=w_raw[:].rearrange("p (u e) c -> p u (e c)", u=2),
+            in_=W.rearrange("(u q e) c -> q u (e c)", u=2, e=2),
+        )
+        nd = [keep.tile([P, RT, F], BF16, name="nd%d" % b) for b in range(B)]
+        for j in range(4):
+            nc.sync.dma_start(
+                out=nd[0][:, 2 * j : 2 * j + 2, :],
+                in_=nodes[0, 256 * j : 256 * j + 256, :].rearrange("(r p) f -> p r f", p=P),
+            )
+        for b in range(1, B):
+            nc.sync.dma_start(out=nd[b][:], in_=nodes[b].rearrange("(r p) f -> p r f", p=P))
+
+        w_grp = keep.tile([P, 4 * F], BF16, name="w_grp", align_bytes=64)
+        w_cod = keep.tile([P, F], U32, name="w_cod", align_bytes=64)
+        w_scl = keep.tile([P, F], U8, name="w_scl", align_bytes=64)
+        w_view = w_raw[:].rearrange("p t (u m e) -> p t u m e", u=2, e=2)
+        for t in range(4):
+            dst = w_grp[:, 512 * t : 512 * t + 512].rearrange("p (m t) -> p m t", t=4)
+            srcv = w_view[:, :, t // 2, :, t % 2].rearrange("p t m -> p m t")
+            if t == 3:
+                nc.scalar.copy(out=dst, in_=srcv)
+            else:
+                nc.vector.tensor_copy(out=dst, in_=srcv)
+        nc.vector.quantize_mx(out=w_cod[:].bitcast(FP8X4), scales=w_scl[:], in_=w_grp[:])
+
+        n_grp = {}
+        x_grp = {}
+        n_cod = [keep.tile([P, N], U32, name="n_cod%d" % b, align_bytes=64) for b in range(B)]
+        n_scl = [keep.tile([P, N], U8, name="n_scl%d" % b, align_bytes=64) for b in range(B)]
+        x_cod = [keep.tile([P, N], U32, name="x_cod%d" % b, align_bytes=64) for b in range(B)]
+        x_scl = [keep.tile([P, N], U8, name="x_scl%d" % b, align_bytes=64) for b in range(B)]
+        aux = {}
+        pr = {}
+        st = {}
+
+        def aux_tile(tag):
+            if tag == "aux":
+                return ps_aux.tile([P, 4, P], F32, name="aux", tag="aux")
+            return ps_pr.tile([P, 4, P], F32, name=tag, tag=tag)
+
+        def copy(eng, dst, srcv):
+            if eng == "S":
+                nc.scalar.copy(out=dst, in_=srcv)
+            else:
+                nc.vector.tensor_copy(out=dst, in_=srcv)
+
+        def tr(b, j, tag="aux"):
+            if b >= B:
+                return
+            tp = aux_tile(tag)
+            aux[("t", b, j)] = tp
+            for r2 in range(2):
+                words = nd[b][:, 2 * j + r2, :].bitcast(F32)
+                for u in range(2):
+                    nc.tensor.transpose(tp[:, 2 * r2 + u, :], words[:, P * u : P * u + P], ident[:])
+
+        def cp_t(b, j, eng):
+            if b >= B:
+                return
+            if j == 0:
+                n_grp[b] = grp.tile([P, 4 * N], BF16, name="n_grp", tag="n_grp", align_bytes=64)
+            tp = aux[("t", b, j)]
+            dst = n_grp[b][:, 1024 * j : 1024 * j + 1024].bitcast(F32)
+            copy(
+                eng,
+                dst.rearrange("p (r n u) -> p r n u", r=2, u=2),
+                tp[:].rearrange("p (r u) n -> p r n u", r=2),
+            )
+
+        def qn(b, h):
+            if b >= B:
+                return
+            cols = slice(512 * h, 512 * h + 512)
+            nc.vector.quantize_mx(
+                out=n_cod[b][:, cols].bitcast(FP8X4),
+                scales=n_scl[b][:, cols],
+                in_=n_grp[b][:, 2048 * h : 2048 * h + 2048],
+            )
+
+        def m1(b, c, tag="aux"):
+            if b >= B:
+                return
+            px = aux_tile(tag)
+            aux[("x", b, c)] = px
+            cols = slice(P * c, P * c + P)
+            for t in range(4):
+                wc = slice(P * t, P * t + P)
+                nc.tensor.matmul_mx(
+                    out=px[:, t, :],
+                    lhsT=w_cod[:, wc].bitcast(FP8X4),
+                    lhsT_scale=w_scl[:, wc],
+                    rhs=n_cod[b][:, cols].bitcast(FP8X4),
+                    rhs_scale=n_scl[b][:, cols],
+                    start=True,
+                    stop=True,
+                )
+
+        def cp_x(b, c, eng):
+            if b >= B:
+                return
+            if c == 0:
+                x_grp[b] = grp.tile([P, 4 * N], BF16, name="x_grp", tag="x_grp", align_bytes=64)
+            px = aux[("x", b, c)]
+            copy(
+                eng,
+                x_grp[b][:, 512 * c : 512 * c + 512].rearrange("p (n t) -> p n t", t=4),
+                px[:].rearrange("p t n -> p n t"),
+            )
+
+        def qx(b, h):
+            if b >= B:
+                return
+            cols = slice(512 * h, 512 * h + 512)
+            nc.vector.quantize_mx(
+                out=x_cod[b][:, cols].bitcast(FP8X4),
+                scales=x_scl[b][:, cols],
+                in_=x_grp[b][:, 2048 * h : 2048 * h + 2048],
+            )
+
+        def m2(i):
+            if i >= NT:
+                return
+            b, r = divmod(i, RT)
+            rows = slice(P * r, P * r + P)
+            banks = []
+            for h in range(2):
+                tag = "prA" if h == 0 else "prB"
+                pt = ps_pr.tile([P, 512], F32, name=tag, tag=tag)
+                cols = slice(512 * h, 512 * h + 512)
+                nc.tensor.matmul_mx(
+                    out=pt[:],
+                    lhsT=x_cod[b][:, rows].bitcast(FP8X4),
+                    lhsT_scale=x_scl[b][:, rows],
+                    rhs=n_cod[b][:, cols].bitcast(FP8X4),
+                    rhs_scale=n_scl[b][:, cols],
+                    start=True,
+                    stop=True,
+                )
+                banks.append(pt)
+            pr[i] = banks
+
+        def mx(i):
+            if i >= NT:
+                return
+            m = small.tile([P, 2], F32, name="m", tag="m")
+            for h in range(2):
+                nc.vector.tensor_reduce(out=m[:, h : h + 1], in_=pr[i][h][:], axis=AX.X, op=ALU.max)
+            nb = small.tile([P, 1], F32, name="nb", tag="nb")
+            nc.vector.tensor_scalar(
+                out=nb[:], in0=m[:, 0:1], scalar1=m[:, 1:2], scalar2=-NORM, op0=ALU.max, op1=ALU.mult
+            )
+            st[("nb", i)] = nb
+
+        def ex(i):
+            e = epool.tile([P, N], F32, name="e", tag="e")
+            ss = small.tile([P, 2], F32, name="ss", tag="ss")
+            for h in range(2):
+                nc.scalar.activation(
+                    out=e[:, 512 * h : 512 * h + 512],
+                    in_=pr[i][h][:],
+                    func=ACT.Exp,
+                    bias=st[("nb", i)][:],
+                    scale=NORM,
+                    accum_out=ss[:, h : h + 1],
+                )
+            st[("e", i)] = e
+            st[("ss", i)] = ss
+
+        def fin(i):
+            if i < 0:
+                return
+            b, r = divmod(i, RT)
+            ss = st[("ss", i)]
+            e = st[("e", i)]
+            tot = small.tile([P, 1], F32, name="tot", tag="tot")
+            nc.vector.tensor_tensor(out=tot[:], in0=ss[:, 0:1], in1=ss[:, 1:2], op=ALU.add)
+            rr = small.tile([P, 1], F32, name="rr", tag="rr")
+            nc.vector.reciprocal(out=rr[:], in_=tot[:])
+            nc.gpsimd.tensor_scalar(
+                out=e[:], in0=e[:], scalar1=rr[:], scalar2=0.0, op0=ALU.mult, op1=ALU.add
+            )
+            nc.sync.dma_start(out=out[b, P * r : P * r + P, :], in_=e[:])
+
+        tr(0, 0, "aux")
+        tr(0, 1, "aux")
+        tr(0, 2, "prA")
+        tr(0, 3, "prB")
+        cp_t(0, 0, "S")
+        cp_t(0, 1, "V")
+        qn(0, 0)
+        cp_t(0, 2, "S")
+        cp_t(0, 3, "V")
+        m1(0, 0, "prA")
+        m1(0, 1, "prB")
+        m1(0, 2, "prA")
+        m1(0, 3, "prB")
+        cp_x(0, 0, "S")
+        cp_x(0, 1, "V")
+        qn(0, 1)
+        cp_x(0, 2, "S")
+        cp_x(0, 3, "V")
+        m1(0, 4, "aux")
+        m1(0, 5, "aux")
+        qx(0, 0)
+        m2(0)
+        m2(1)
+        mx(0)
+        cp_x(0, 4, "S")
+        cp_x(0, 5, "V")
+        m1(0, 6, "aux")
+        m1(0, 7, "aux")
+        cp_x(0, 6, "S")
+        cp_x(0, 7, "V")
+        tr(1, 0)
+        tr(1, 1)
+        cp_t(1, 0, "S")
+        cp_t(1, 1, "V")
+        qn(1, 0)
+        m1(1, 0)
+
+        for s in range(NT):
+            b, r = divmod(s, RT)
+            nx = b + 1
+            m2(s + 2)
+            mx(s + 1)
+            ex(s)
+            fin(s - 1)
+            if r == 0:
+                qx(b, 1)
+                tr(nx, 2)
+            elif r == 1:
+                cp_t(nx, 2, "V")
+                tr(nx, 3)
+            elif r == 2:
+                cp_t(nx, 3, "V")
+            elif r == 3:
+                qn(nx, 1)
+            elif r == 4:
+                qx(nx, 0)
+                tr(nx + 1, 0)
+            elif r == 5:
+                cp_t(nx + 1, 0, "V")
+                tr(nx + 1, 1)
+            elif r == 6:
+                cp_t(nx + 1, 1, "V")
+            else:
+                qn(nx + 1, 0)
+            cp_x(nx, r, "S")
+            if r < RT - 1:
+                m1(nx, r + 1)
+            else:
+                m1(nx + 1, 0)
+        fin(NT - 1)

@@ -18,6 +18,8 @@ P = 128
 RT = N // P
 NT = B * RT
 NORM = 1.0 / math.sqrt(F)
+LAST_BATCH_FIRST = NT - RT
+S_SHARE_FROM = 576
 FLOPS = 2 * B * (N * F * F + N * N * F)
 
 
@@ -218,9 +220,12 @@ def tile_scalarproductattentiont_pa_t_kernel(tc, nodes, W, out):
             nc.vector.tensor_tensor(out=tot[:], in0=ss[:, 0:1], in1=ss[:, 1:2], op=ALU.add)
             rr = small.tile([P, 1], F32, name="rr", tag="rr")
             nc.vector.reciprocal(out=rr[:], in_=tot[:])
-            nc.gpsimd.tensor_scalar(
-                out=e[:], in0=e[:], scalar1=rr[:], scalar2=0.0, op0=ALU.mult, op1=ALU.add
+            split = S_SHARE_FROM if i >= LAST_BATCH_FIRST else N
+            nc.vector.tensor_scalar(
+                out=e[:, 0:split], in0=e[:, 0:split], scalar1=rr[:], scalar2=None, op0=ALU.mult
             )
+            if split < N:
+                nc.scalar.activation(out=e[:, split:N], in_=e[:, split:N], func=ACT.Copy, scale=rr[:])
             nc.sync.dma_start(out=out[b, P * r : P * r + P, :], in_=e[:])
 
         tr(0, 0, "aux")
@@ -269,27 +274,31 @@ def tile_scalarproductattentiont_pa_t_kernel(tc, nodes, W, out):
             fin(s - 1)
             if r == 0:
                 qx(b, 1)
-                tr(nx, 2)
-            elif r == 1:
-                cp_t(nx, 2, "V")
-                tr(nx, 3)
-            elif r == 2:
-                cp_t(nx, 3, "V")
             elif r == 3:
                 qn(nx, 1)
             elif r == 4:
                 qx(nx, 0)
-                tr(nx + 1, 0)
-            elif r == 5:
-                cp_t(nx + 1, 0, "V")
-                tr(nx + 1, 1)
-            elif r == 6:
-                cp_t(nx + 1, 1, "V")
-            else:
+            elif r == 7:
                 qn(nx + 1, 0)
             cp_x(nx, r, "S")
+            if r == 1:
+                cp_t(nx, 2, "S")
+            elif r == 2:
+                cp_t(nx, 3, "S")
+            elif r == 5:
+                cp_t(nx + 1, 0, "S")
+            elif r == 6:
+                cp_t(nx + 1, 1, "S")
             if r < RT - 1:
                 m1(nx, r + 1)
             else:
                 m1(nx + 1, 0)
+            if r == 0:
+                tr(nx, 2)
+            elif r == 1:
+                tr(nx, 3)
+            elif r == 4:
+                tr(nx + 1, 0)
+            elif r == 5:
+                tr(nx + 1, 1)
         fin(NT - 1)

@@ -18,9 +18,14 @@ P = 128
 RT = N // P
 NT = B * RT
 NORM = 1.0 / math.sqrt(F)
-LAST_BATCH_FIRST = NT - RT
-S_SHARE_FROM = 576
 FLOPS = 2 * B * (N * F * F + N * N * F)
+
+MANUAL = True
+NRM_G = True
+ACCUM_MAX = True
+S_FROM_LAST = 576
+S_FROM = 1024
+V_CPT = [1,5]
 
 
 def tile_scalarproductattentiont_pa_t_kernel(tc, nodes, W, out):
@@ -28,10 +33,12 @@ def tile_scalarproductattentiont_pa_t_kernel(tc, nodes, W, out):
     with ExitStack() as ctx:
         keep = ctx.enter_context(tc.tile_pool(name="keep", bufs=1))
         grp = ctx.enter_context(tc.tile_pool(name="grp", bufs=2))
-        epool = ctx.enter_context(tc.tile_pool(name="epool", bufs=10))
+        epool = ctx.enter_context(tc.tile_pool(name="epool", bufs=8))
         small = ctx.enter_context(tc.tile_pool(name="small", bufs=8))
         ps_pr = ctx.enter_context(tc.psum_pool(name="ps_pr", bufs=3))
         ps_aux = ctx.enter_context(tc.psum_pool(name="ps_aux", bufs=2))
+        if MANUAL:
+            ctx.enter_context(tc.manual_schedule())
 
         ident = keep.tile([P, P], F32, name="ident")
         make_identity(nc, ident[:])
@@ -57,15 +64,7 @@ def tile_scalarproductattentiont_pa_t_kernel(tc, nodes, W, out):
         w_grp = keep.tile([P, 4 * F], BF16, name="w_grp", align_bytes=64)
         w_cod = keep.tile([P, F], U32, name="w_cod", align_bytes=64)
         w_scl = keep.tile([P, F], U8, name="w_scl", align_bytes=64)
-        w_view = w_raw[:].rearrange("p t (u m e) -> p t u m e", u=2, e=2)
-        for t in range(4):
-            dst = w_grp[:, 512 * t : 512 * t + 512].rearrange("p (m t) -> p m t", t=4)
-            srcv = w_view[:, :, t // 2, :, t % 2].rearrange("p t m -> p m t")
-            if t == 3:
-                nc.scalar.copy(out=dst, in_=srcv)
-            else:
-                nc.vector.tensor_copy(out=dst, in_=srcv)
-        nc.vector.quantize_mx(out=w_cod[:].bitcast(FP8X4), scales=w_scl[:], in_=w_grp[:])
+        junk = keep.tile([P, 512], F32, name="junk") if ACCUM_MAX else None
 
         n_grp = {}
         x_grp = {}
@@ -87,6 +86,17 @@ def tile_scalarproductattentiont_pa_t_kernel(tc, nodes, W, out):
                 nc.scalar.copy(out=dst, in_=srcv)
             else:
                 nc.vector.tensor_copy(out=dst, in_=srcv)
+
+        def w_piece(t, eng):
+            w_view = w_raw[:].rearrange("p t (u m e) -> p t u m e", u=2, e=2)
+            copy(
+                eng,
+                w_grp[:, 512 * t : 512 * t + 512].rearrange("p (m t) -> p m t", t=4),
+                w_view[:, :, t // 2, :, t % 2].rearrange("p t m -> p m t"),
+            )
+
+        def w_quant():
+            nc.vector.quantize_mx(out=w_cod[:].bitcast(FP8X4), scales=w_scl[:], in_=w_grp[:])
 
         def tr(b, j, tag="aux"):
             if b >= B:
@@ -111,15 +121,21 @@ def tile_scalarproductattentiont_pa_t_kernel(tc, nodes, W, out):
                 tp[:].rearrange("p (r u) n -> p r n u", r=2),
             )
 
-        def qn(b, h):
+        def quant(b, cod, scl, grouped, q0, nq):
             if b >= B:
                 return
-            cols = slice(512 * h, 512 * h + 512)
+            cols = slice(256 * q0, 256 * (q0 + nq))
             nc.vector.quantize_mx(
-                out=n_cod[b][:, cols].bitcast(FP8X4),
-                scales=n_scl[b][:, cols],
-                in_=n_grp[b][:, 2048 * h : 2048 * h + 2048],
+                out=cod[b][:, cols].bitcast(FP8X4),
+                scales=scl[b][:, cols],
+                in_=grouped[b][:, 1024 * q0 : 1024 * (q0 + nq)],
             )
+
+        def qn(b, q0, nq):
+            quant(b, n_cod, n_scl, n_grp, q0, nq)
+
+        def qx(b, q0, nq):
+            quant(b, x_cod, x_scl, x_grp, q0, nq)
 
         def m1(b, c, tag="aux"):
             if b >= B:
@@ -151,16 +167,6 @@ def tile_scalarproductattentiont_pa_t_kernel(tc, nodes, W, out):
                 px[:].rearrange("p t n -> p n t"),
             )
 
-        def qx(b, h):
-            if b >= B:
-                return
-            cols = slice(512 * h, 512 * h + 512)
-            nc.vector.quantize_mx(
-                out=x_cod[b][:, cols].bitcast(FP8X4),
-                scales=x_scl[b][:, cols],
-                in_=x_grp[b][:, 2048 * h : 2048 * h + 2048],
-            )
-
         def m2(i):
             if i >= NT:
                 return
@@ -186,13 +192,24 @@ def tile_scalarproductattentiont_pa_t_kernel(tc, nodes, W, out):
         def mx(i):
             if i >= NT:
                 return
-            m = small.tile([P, 2], F32, name="m", tag="m")
-            for h in range(2):
-                nc.vector.tensor_reduce(out=m[:, h : h + 1], in_=pr[i][h][:], axis=AX.X, op=ALU.max)
             nb = small.tile([P, 1], F32, name="nb", tag="nb")
-            nc.vector.tensor_scalar(
-                out=nb[:], in0=m[:, 0:1], scalar1=m[:, 1:2], scalar2=-NORM, op0=ALU.max, op1=ALU.mult
-            )
+            if ACCUM_MAX:
+                na = small.tile([P, 1], F32, name="na", tag="na")
+                nc.vector.tensor_scalar(
+                    out=junk[:], in0=pr[i][0][:], scalar1=-NORM, scalar2=None,
+                    op0=ALU.mult, op1=ALU.min, accum_out=na[:],
+                )
+                nc.vector.tensor_scalar(
+                    out=junk[:], in0=pr[i][1][:], scalar1=-NORM, scalar2=na[:],
+                    op0=ALU.mult, op1=ALU.min, accum_out=nb[:],
+                )
+            else:
+                m = small.tile([P, 2], F32, name="m", tag="m")
+                for h in range(2):
+                    nc.vector.tensor_reduce(out=m[:, h : h + 1], in_=pr[i][h][:], axis=AX.X, op=ALU.max)
+                nc.vector.tensor_scalar(
+                    out=nb[:], in0=m[:, 0:1], scalar1=m[:, 1:2], scalar2=-NORM, op0=ALU.max, op1=ALU.mult
+                )
             st[("nb", i)] = nb
 
         def ex(i):
@@ -210,85 +227,112 @@ def tile_scalarproductattentiont_pa_t_kernel(tc, nodes, W, out):
             st[("e", i)] = e
             st[("ss", i)] = ss
 
-        def fin(i):
+        def sums(i):
+            if i < 0:
+                return
+            tot = small.tile([P, 1], F32, name="tot", tag="tot")
+            nc.vector.tensor_reduce(out=tot[:], in_=st[("ss", i)][:], axis=AX.X, op=ALU.add)
+            rr = small.tile([P, 1], F32, name="rr", tag="rr")
+            nc.vector.reciprocal(out=rr[:], in_=tot[:])
+            st[("rr", i)] = rr
+
+        def nrm(i, on_g, s_from):
             if i < 0:
                 return
             b, r = divmod(i, RT)
-            ss = st[("ss", i)]
             e = st[("e", i)]
-            tot = small.tile([P, 1], F32, name="tot", tag="tot")
-            nc.vector.tensor_tensor(out=tot[:], in0=ss[:, 0:1], in1=ss[:, 1:2], op=ALU.add)
-            rr = small.tile([P, 1], F32, name="rr", tag="rr")
-            nc.vector.reciprocal(out=rr[:], in_=tot[:])
-            split = S_SHARE_FROM if i >= LAST_BATCH_FIRST else N
-            nc.vector.tensor_scalar(
-                out=e[:, 0:split], in0=e[:, 0:split], scalar1=rr[:], scalar2=None, op0=ALU.mult
-            )
-            if split < N:
-                nc.scalar.activation(out=e[:, split:N], in_=e[:, split:N], func=ACT.Copy, scale=rr[:])
+            rr = st[("rr", i)]
+            if on_g:
+                nc.gpsimd.tensor_scalar(
+                    out=e[:], in0=e[:], scalar1=rr[:], scalar2=0.0, op0=ALU.mult, op1=ALU.add
+                )
+            else:
+                nc.vector.tensor_scalar(
+                    out=e[:, 0:s_from], in0=e[:, 0:s_from], scalar1=rr[:], scalar2=None, op0=ALU.mult
+                )
+                if s_from < N:
+                    nc.scalar.activation(
+                        out=e[:, s_from:N], in_=e[:, s_from:N], func=ACT.Copy, scale=rr[:]
+                    )
             nc.sync.dma_start(out=out[b, P * r : P * r + P, :], in_=e[:])
 
         tr(0, 0, "aux")
         tr(0, 1, "aux")
         tr(0, 2, "prA")
-        tr(0, 3, "prB")
+        w_piece(0, "V")
+        w_piece(1, "V")
+        w_piece(2, "V")
+        w_piece(3, "S")
+        w_quant()
         cp_t(0, 0, "S")
+        qn(0, 0, 1)
         cp_t(0, 1, "V")
-        qn(0, 0)
+        m1(0, 0, "prB")
+        m1(0, 1, "prA")
+        tr(0, 3, "prB")
+        qn(0, 1, 1)
         cp_t(0, 2, "S")
-        cp_t(0, 3, "V")
-        m1(0, 0, "prA")
-        m1(0, 1, "prB")
+        cp_x(0, 0, "V")
+        cp_x(0, 1, "S")
         m1(0, 2, "prA")
         m1(0, 3, "prB")
-        cp_x(0, 0, "S")
-        cp_x(0, 1, "V")
-        qn(0, 1)
-        cp_x(0, 2, "S")
-        cp_x(0, 3, "V")
+        qn(0, 2, 1)
+        cp_t(0, 3, "S")
+        qx(0, 0, 1)
+        qn(0, 3, 1)
+        m2(0)
         m1(0, 4, "aux")
         m1(0, 5, "aux")
-        qx(0, 0)
-        m2(0)
+        cp_x(0, 2, "V")
+        cp_x(0, 3, "S")
         m2(1)
-        mx(0)
-        cp_x(0, 4, "S")
-        cp_x(0, 5, "V")
+        cp_x(0, 4, "V")
+        cp_x(0, 5, "S")
         m1(0, 6, "aux")
         m1(0, 7, "aux")
-        cp_x(0, 6, "S")
-        cp_x(0, 7, "V")
+        qx(0, 1, 1)
+        cp_x(0, 6, "V")
+        cp_x(0, 7, "S")
         tr(1, 0)
         tr(1, 1)
+        mx(0)
         cp_t(1, 0, "S")
-        cp_t(1, 1, "V")
-        qn(1, 0)
+        cp_t(1, 1, "S")
+        qn(1, 0, 2)
         m1(1, 0)
 
         for s in range(NT):
             b, r = divmod(s, RT)
             nx = b + 1
+            last = s - 1 >= NT - RT
             m2(s + 2)
-            mx(s + 1)
+            if NRM_G:
+                sums(s - 1)
+                nrm(s - 1, True, N)
+                mx(s + 1)
+            else:
+                mx(s + 1)
+                sums(s - 1)
+                nrm(s - 1, False, S_FROM_LAST if last else S_FROM)
             ex(s)
-            fin(s - 1)
             if r == 0:
-                qx(b, 1)
+                qx(b, 2, 2)
             elif r == 3:
-                qn(nx, 1)
+                qn(nx, 2, 2)
             elif r == 4:
-                qx(nx, 0)
+                qx(nx, 0, 2)
             elif r == 7:
-                qn(nx + 1, 0)
+                qn(nx + 1, 0, 2)
             cp_x(nx, r, "S")
+            eng = "V" if r in V_CPT else "S"
             if r == 1:
-                cp_t(nx, 2, "S")
+                cp_t(nx, 2, eng)
             elif r == 2:
-                cp_t(nx, 3, "S")
+                cp_t(nx, 3, eng)
             elif r == 5:
-                cp_t(nx + 1, 0, "S")
+                cp_t(nx + 1, 0, eng)
             elif r == 6:
-                cp_t(nx + 1, 1, "S")
+                cp_t(nx + 1, 1, eng)
             if r < RT - 1:
                 m1(nx, r + 1)
             else:
@@ -301,4 +345,5 @@ def tile_scalarproductattentiont_pa_t_kernel(tc, nodes, W, out):
                 tr(nx + 1, 0)
             elif r == 5:
                 tr(nx + 1, 1)
-        fin(NT - 1)
+        sums(NT - 1)
+        nrm(NT - 1, False, S_FROM_LAST)

@@ -20,12 +20,13 @@ NT = B * RT
 NORM = 1.0 / math.sqrt(F)
 FLOPS = 2 * B * (N * F * F + N * N * F)
 
-MANUAL = True
-NRM_G = True
-ACCUM_MAX = True
+SINGLES = 2
+MANUAL = False
+NRM_G = False
+ACCUM_MAX = False
 S_FROM_LAST = 576
 S_FROM = 1024
-V_CPT = [1,5]
+V_CPT = []
 
 
 def tile_scalarproductattentiont_pa_t_kernel(tc, nodes, W, out):
@@ -212,9 +213,17 @@ def tile_scalarproductattentiont_pa_t_kernel(tc, nodes, W, out):
                 )
             st[("nb", i)] = nb
 
+        def group_of(i):
+            if i >= NT - SINGLES:
+                return i, 1
+            return i - i % 2, 2
+
         def ex(i):
+            g0, gn = group_of(i)
             e = epool.tile([P, N], F32, name="e", tag="e")
-            ss = small.tile([P, 2], F32, name="ss", tag="ss")
+            if i == g0:
+                st[("ss", g0)] = small.tile([P, gn, 2], F32, name="ss", tag="ss")
+            ss = st[("ss", g0)]
             for h in range(2):
                 nc.scalar.activation(
                     out=e[:, 512 * h : 512 * h + 512],
@@ -222,39 +231,44 @@ def tile_scalarproductattentiont_pa_t_kernel(tc, nodes, W, out):
                     func=ACT.Exp,
                     bias=st[("nb", i)][:],
                     scale=NORM,
-                    accum_out=ss[:, h : h + 1],
+                    accum_out=ss[:, i - g0, h : h + 1],
                 )
             st[("e", i)] = e
-            st[("ss", i)] = ss
 
-        def sums(i):
-            if i < 0:
-                return
-            tot = small.tile([P, 1], F32, name="tot", tag="tot")
-            nc.vector.tensor_reduce(out=tot[:], in_=st[("ss", i)][:], axis=AX.X, op=ALU.add)
-            rr = small.tile([P, 1], F32, name="rr", tag="rr")
+        def sums(g0):
+            gn = group_of(g0)[1]
+            tot = small.tile([P, gn], F32, name="tot", tag="tot")
+            nc.vector.tensor_reduce(out=tot[:], in_=st[("ss", g0)][:], axis=AX.X, op=ALU.add)
+            rr = small.tile([P, gn], F32, name="rr", tag="rr")
             nc.vector.reciprocal(out=rr[:], in_=tot[:])
-            st[("rr", i)] = rr
+            st[("rr", g0)] = rr
 
-        def nrm(i, on_g, s_from):
-            if i < 0:
-                return
+        def nrm(i, s_from):
             b, r = divmod(i, RT)
+            g0 = group_of(i)[0]
             e = st[("e", i)]
-            rr = st[("rr", i)]
-            if on_g:
-                nc.gpsimd.tensor_scalar(
-                    out=e[:], in0=e[:], scalar1=rr[:], scalar2=0.0, op0=ALU.mult, op1=ALU.add
-                )
-            else:
-                nc.vector.tensor_scalar(
-                    out=e[:, 0:s_from], in0=e[:, 0:s_from], scalar1=rr[:], scalar2=None, op0=ALU.mult
-                )
-                if s_from < N:
-                    nc.scalar.activation(
-                        out=e[:, s_from:N], in_=e[:, s_from:N], func=ACT.Copy, scale=rr[:]
-                    )
+            rr = st[("rr", g0)][:, i - g0 : i - g0 + 1]
+            nc.vector.tensor_scalar(
+                out=e[:, 0:s_from], in0=e[:, 0:s_from], scalar1=rr, scalar2=None, op0=ALU.mult
+            )
+            if s_from < N:
+                nc.scalar.activation(out=e[:, s_from:N], in_=e[:, s_from:N], func=ACT.Copy, scale=rr)
             nc.sync.dma_start(out=out[b, P * r : P * r + P, :], in_=e[:])
+
+        done = []
+
+        def finish(upto, s_from, most):
+            k = 0
+            while len(done) <= upto and k < most:
+                i = len(done)
+                g0, gn = group_of(i)
+                if g0 + gn - 1 > upto:
+                    return
+                if i == g0:
+                    sums(g0)
+                nrm(i, s_from)
+                done.append(i)
+                k += 1
 
         tr(0, 0, "aux")
         tr(0, 1, "aux")
@@ -291,6 +305,7 @@ def tile_scalarproductattentiont_pa_t_kernel(tc, nodes, W, out):
         m1(0, 6, "aux")
         m1(0, 7, "aux")
         qx(0, 1, 1)
+        m2(2)
         cp_x(0, 6, "V")
         cp_x(0, 7, "S")
         tr(1, 0)
@@ -304,17 +319,10 @@ def tile_scalarproductattentiont_pa_t_kernel(tc, nodes, W, out):
         for s in range(NT):
             b, r = divmod(s, RT)
             nx = b + 1
-            last = s - 1 >= NT - RT
-            m2(s + 2)
-            if NRM_G:
-                sums(s - 1)
-                nrm(s - 1, True, N)
-                mx(s + 1)
-            else:
-                mx(s + 1)
-                sums(s - 1)
-                nrm(s - 1, False, S_FROM_LAST if last else S_FROM)
+            mx(s + 1)
+            finish(s - 1, S_FROM_LAST if s >= NT - RT else S_FROM, 2 if s >= NT - 2 else 1)
             ex(s)
+            m2(s + 3)
             if r == 0:
                 qx(b, 2, 2)
             elif r == 3:
@@ -345,5 +353,4 @@ def tile_scalarproductattentiont_pa_t_kernel(tc, nodes, W, out):
                 tr(nx + 1, 0)
             elif r == 5:
                 tr(nx + 1, 1)
-        sums(NT - 1)
-        nrm(NT - 1, False, S_FROM_LAST)
+        finish(NT - 1, S_FROM_LAST, NT)

@@ -20,6 +20,7 @@ NT = B * RT
 NORM = 1.0 / math.sqrt(F)
 FLOPS = 2 * B * (N * F * F + N * N * F)
 
+GROUP = 2
 SINGLES = 2
 MANUAL = False
 NRM_G = False
@@ -34,10 +35,10 @@ def tile_scalarproductattentiont_pa_t_kernel(tc, nodes, W, out):
     with ExitStack() as ctx:
         keep = ctx.enter_context(tc.tile_pool(name="keep", bufs=1))
         grp = ctx.enter_context(tc.tile_pool(name="grp", bufs=2))
-        epool = ctx.enter_context(tc.tile_pool(name="epool", bufs=8))
+        epool = ctx.enter_context(tc.tile_pool(name="epool", bufs=12))
         small = ctx.enter_context(tc.tile_pool(name="small", bufs=8))
-        ps_pr = ctx.enter_context(tc.psum_pool(name="ps_pr", bufs=3))
-        ps_aux = ctx.enter_context(tc.psum_pool(name="ps_aux", bufs=2))
+        ps_pr = ctx.enter_context(tc.psum_pool(name="ps_pr", bufs=2))
+        ps_aux = ctx.enter_context(tc.psum_pool(name="ps_aux", bufs=4))
         if MANUAL:
             ctx.enter_context(tc.manual_schedule())
 
@@ -190,57 +191,43 @@ def tile_scalarproductattentiont_pa_t_kernel(tc, nodes, W, out):
                 banks.append(pt)
             pr[i] = banks
 
-        def mx(i):
-            if i >= NT:
-                return
-            nb = small.tile([P, 1], F32, name="nb", tag="nb")
-            if ACCUM_MAX:
-                na = small.tile([P, 1], F32, name="na", tag="na")
-                nc.vector.tensor_scalar(
-                    out=junk[:], in0=pr[i][0][:], scalar1=-NORM, scalar2=None,
-                    op0=ALU.mult, op1=ALU.min, accum_out=na[:],
-                )
-                nc.vector.tensor_scalar(
-                    out=junk[:], in0=pr[i][1][:], scalar1=-NORM, scalar2=na[:],
-                    op0=ALU.mult, op1=ALU.min, accum_out=nb[:],
-                )
-            else:
-                m = small.tile([P, 2], F32, name="m", tag="m")
-                for h in range(2):
-                    nc.vector.tensor_reduce(out=m[:, h : h + 1], in_=pr[i][h][:], axis=AX.X, op=ALU.max)
-                nc.vector.tensor_scalar(
-                    out=nb[:], in0=m[:, 0:1], scalar1=m[:, 1:2], scalar2=-NORM, op0=ALU.max, op1=ALU.mult
-                )
-            st[("nb", i)] = nb
-
         def group_of(i):
             if i >= NT - SINGLES:
                 return i, 1
-            return i - i % 2, 2
+            return i - i % GROUP, GROUP
+
+        def mx(i):
+            if i >= NT:
+                return
+            e = epool.tile([P, N], F32, name="e", tag="e")
+            na = small.tile([P, 1], F32, name="na", tag="na")
+            nb = small.tile([P, 1], F32, name="nb", tag="nb")
+            nc.vector.tensor_scalar(
+                out=e[:, 0:512], in0=pr[i][0][:], scalar1=-NORM, scalar2=None,
+                op0=ALU.mult, op1=ALU.min, accum_out=na[:],
+            )
+            nc.vector.tensor_scalar(
+                out=e[:, 512:1024], in0=pr[i][1][:], scalar1=-NORM, scalar2=na[:],
+                op0=ALU.mult, op1=ALU.min, accum_out=nb[:],
+            )
+            st[("nb", i)] = nb
+            st[("e", i)] = e
 
         def ex(i):
             g0, gn = group_of(i)
-            e = epool.tile([P, N], F32, name="e", tag="e")
+            e = st[("e", i)]
             if i == g0:
-                st[("ss", g0)] = small.tile([P, gn, 2], F32, name="ss", tag="ss")
+                st[("ss", g0)] = small.tile([P, gn], F32, name="ss", tag="ss")
             ss = st[("ss", g0)]
-            for h in range(2):
-                nc.scalar.activation(
-                    out=e[:, 512 * h : 512 * h + 512],
-                    in_=pr[i][h][:],
-                    func=ACT.Exp,
-                    bias=st[("nb", i)][:],
-                    scale=NORM,
-                    accum_out=ss[:, i - g0, h : h + 1],
-                )
-            st[("e", i)] = e
+            nc.scalar.activation(
+                out=e[:], in_=e[:], func=ACT.Exp, bias=st[("nb", i)][:], scale=-1.0,
+                accum_out=ss[:, i - g0 : i - g0 + 1],
+            )
 
         def sums(g0):
             gn = group_of(g0)[1]
-            tot = small.tile([P, gn], F32, name="tot", tag="tot")
-            nc.vector.tensor_reduce(out=tot[:], in_=st[("ss", g0)][:], axis=AX.X, op=ALU.add)
             rr = small.tile([P, gn], F32, name="rr", tag="rr")
-            nc.vector.reciprocal(out=rr[:], in_=tot[:])
+            nc.vector.reciprocal(out=rr[:], in_=st[("ss", g0)][:])
             st[("rr", g0)] = rr
 
         def nrm(i, s_from):
@@ -272,7 +259,7 @@ def tile_scalarproductattentiont_pa_t_kernel(tc, nodes, W, out):
 
         tr(0, 0, "aux")
         tr(0, 1, "aux")
-        tr(0, 2, "prA")
+        tr(0, 2, "aux")
         w_piece(0, "V")
         w_piece(1, "V")
         w_piece(2, "V")
@@ -281,9 +268,9 @@ def tile_scalarproductattentiont_pa_t_kernel(tc, nodes, W, out):
         cp_t(0, 0, "S")
         qn(0, 0, 1)
         cp_t(0, 1, "V")
-        m1(0, 0, "prB")
-        m1(0, 1, "prA")
-        tr(0, 3, "prB")
+        m1(0, 0, "prA")
+        m1(0, 1, "prB")
+        tr(0, 3, "aux")
         qn(0, 1, 1)
         cp_t(0, 2, "S")
         cp_x(0, 0, "V")
@@ -305,12 +292,12 @@ def tile_scalarproductattentiont_pa_t_kernel(tc, nodes, W, out):
         m1(0, 6, "aux")
         m1(0, 7, "aux")
         qx(0, 1, 1)
-        m2(2)
         cp_x(0, 6, "V")
         cp_x(0, 7, "S")
         tr(1, 0)
         tr(1, 1)
         mx(0)
+        m2(2)
         cp_t(1, 0, "S")
         cp_t(1, 1, "S")
         qn(1, 0, 2)

@@ -20,7 +20,6 @@ NT = B * RT
 NORM = 1.0 / math.sqrt(F)
 FLOPS = 2 * B * (N * F * F + N * N * F)
 
-GROUP = 2
 SINGLES = 2
 MANUAL = False
 NRM_G = False
@@ -35,10 +34,10 @@ def tile_scalarproductattentiont_pa_t_kernel(tc, nodes, W, out):
     with ExitStack() as ctx:
         keep = ctx.enter_context(tc.tile_pool(name="keep", bufs=1))
         grp = ctx.enter_context(tc.tile_pool(name="grp", bufs=2))
-        epool = ctx.enter_context(tc.tile_pool(name="epool", bufs=12))
+        epool = ctx.enter_context(tc.tile_pool(name="epool", bufs=8))
         small = ctx.enter_context(tc.tile_pool(name="small", bufs=8))
-        ps_pr = ctx.enter_context(tc.psum_pool(name="ps_pr", bufs=2))
-        ps_aux = ctx.enter_context(tc.psum_pool(name="ps_aux", bufs=4))
+        ps_pr = ctx.enter_context(tc.psum_pool(name="ps_pr", bufs=3))
+        ps_aux = ctx.enter_context(tc.psum_pool(name="ps_aux", bufs=2))
         if MANUAL:
             ctx.enter_context(tc.manual_schedule())
 
@@ -58,10 +57,13 @@ def tile_scalarproductattentiont_pa_t_kernel(tc, nodes, W, out):
         for j in range(4):
             nc.sync.dma_start(
                 out=nd[0][:, 2 * j : 2 * j + 2, :],
-                in_=nodes[0, 256 * j : 256 * j + 256, :].rearrange("(r p) f -> p r f", p=P),
+                in_=nodes[0, 256 * j : 256 * j + 256, :].rearrange("(p r) f -> p r f", r=2),
             )
         for b in range(1, B):
-            nc.sync.dma_start(out=nd[b][:], in_=nodes[b].rearrange("(r p) f -> p r f", p=P))
+            nc.sync.dma_start(
+                out=nd[b][:].rearrange("p (j r) f -> p j (r f)", r=2),
+                in_=nodes[b].rearrange("(j p r) f -> p j (r f)", p=P, r=2),
+            )
 
         w_grp = keep.tile([P, 4 * F], BF16, name="w_grp", align_bytes=64)
         w_cod = keep.tile([P, F], U32, name="w_cod", align_bytes=64)
@@ -119,8 +121,8 @@ def tile_scalarproductattentiont_pa_t_kernel(tc, nodes, W, out):
             dst = n_grp[b][:, 1024 * j : 1024 * j + 1024].bitcast(F32)
             copy(
                 eng,
-                dst.rearrange("p (r n u) -> p r n u", r=2, u=2),
-                tp[:].rearrange("p (r u) n -> p r n u", r=2),
+                dst.rearrange("p (n r u) -> p n r u", r=2, u=2),
+                tp[:].rearrange("p (r u) n -> p n r u", r=2),
             )
 
         def quant(b, cod, scl, grouped, q0, nq):
@@ -191,43 +193,57 @@ def tile_scalarproductattentiont_pa_t_kernel(tc, nodes, W, out):
                 banks.append(pt)
             pr[i] = banks
 
-        def group_of(i):
-            if i >= NT - SINGLES:
-                return i, 1
-            return i - i % GROUP, GROUP
-
         def mx(i):
             if i >= NT:
                 return
-            e = epool.tile([P, N], F32, name="e", tag="e")
-            na = small.tile([P, 1], F32, name="na", tag="na")
             nb = small.tile([P, 1], F32, name="nb", tag="nb")
-            nc.vector.tensor_scalar(
-                out=e[:, 0:512], in0=pr[i][0][:], scalar1=-NORM, scalar2=None,
-                op0=ALU.mult, op1=ALU.min, accum_out=na[:],
-            )
-            nc.vector.tensor_scalar(
-                out=e[:, 512:1024], in0=pr[i][1][:], scalar1=-NORM, scalar2=na[:],
-                op0=ALU.mult, op1=ALU.min, accum_out=nb[:],
-            )
+            if ACCUM_MAX:
+                na = small.tile([P, 1], F32, name="na", tag="na")
+                nc.vector.tensor_scalar(
+                    out=junk[:], in0=pr[i][0][:], scalar1=-NORM, scalar2=None,
+                    op0=ALU.mult, op1=ALU.min, accum_out=na[:],
+                )
+                nc.vector.tensor_scalar(
+                    out=junk[:], in0=pr[i][1][:], scalar1=-NORM, scalar2=na[:],
+                    op0=ALU.mult, op1=ALU.min, accum_out=nb[:],
+                )
+            else:
+                m = small.tile([P, 2], F32, name="m", tag="m")
+                for h in range(2):
+                    nc.vector.tensor_reduce(out=m[:, h : h + 1], in_=pr[i][h][:], axis=AX.X, op=ALU.max)
+                nc.vector.tensor_scalar(
+                    out=nb[:], in0=m[:, 0:1], scalar1=m[:, 1:2], scalar2=-NORM, op0=ALU.max, op1=ALU.mult
+                )
             st[("nb", i)] = nb
-            st[("e", i)] = e
+
+        def group_of(i):
+            if i >= NT - SINGLES:
+                return i, 1
+            return i - i % 2, 2
 
         def ex(i):
             g0, gn = group_of(i)
-            e = st[("e", i)]
+            e = epool.tile([P, N], F32, name="e", tag="e")
             if i == g0:
-                st[("ss", g0)] = small.tile([P, gn], F32, name="ss", tag="ss")
+                st[("ss", g0)] = small.tile([P, gn, 2], F32, name="ss", tag="ss")
             ss = st[("ss", g0)]
-            nc.scalar.activation(
-                out=e[:], in_=e[:], func=ACT.Exp, bias=st[("nb", i)][:], scale=-1.0,
-                accum_out=ss[:, i - g0 : i - g0 + 1],
-            )
+            for h in range(2):
+                nc.scalar.activation(
+                    out=e[:, 512 * h : 512 * h + 512],
+                    in_=pr[i][h][:],
+                    func=ACT.Exp,
+                    bias=st[("nb", i)][:],
+                    scale=NORM,
+                    accum_out=ss[:, i - g0, h : h + 1],
+                )
+            st[("e", i)] = e
 
         def sums(g0):
             gn = group_of(g0)[1]
+            tot = small.tile([P, gn], F32, name="tot", tag="tot")
+            nc.vector.tensor_reduce(out=tot[:], in_=st[("ss", g0)][:], axis=AX.X, op=ALU.add)
             rr = small.tile([P, gn], F32, name="rr", tag="rr")
-            nc.vector.reciprocal(out=rr[:], in_=st[("ss", g0)][:])
+            nc.vector.reciprocal(out=rr[:], in_=tot[:])
             st[("rr", g0)] = rr
 
         def nrm(i, s_from):
@@ -259,21 +275,21 @@ def tile_scalarproductattentiont_pa_t_kernel(tc, nodes, W, out):
 
         tr(0, 0, "aux")
         tr(0, 1, "aux")
-        tr(0, 2, "aux")
+        tr(0, 2, "prA")
         w_piece(0, "V")
         w_piece(1, "V")
-        w_piece(2, "V")
+        w_piece(2, "S")
         w_piece(3, "S")
         w_quant()
         cp_t(0, 0, "S")
         qn(0, 0, 1)
-        cp_t(0, 1, "V")
-        m1(0, 0, "prA")
-        m1(0, 1, "prB")
-        tr(0, 3, "aux")
+        cp_t(0, 1, "S")
+        m1(0, 0, "prB")
+        m1(0, 1, "prA")
+        tr(0, 3, "prB")
         qn(0, 1, 1)
         cp_t(0, 2, "S")
-        cp_x(0, 0, "V")
+        cp_x(0, 0, "S")
         cp_x(0, 1, "S")
         m1(0, 2, "prA")
         m1(0, 3, "prB")
@@ -284,20 +300,20 @@ def tile_scalarproductattentiont_pa_t_kernel(tc, nodes, W, out):
         m2(0)
         m1(0, 4, "aux")
         m1(0, 5, "aux")
-        cp_x(0, 2, "V")
+        cp_x(0, 2, "S")
         cp_x(0, 3, "S")
         m2(1)
-        cp_x(0, 4, "V")
+        cp_x(0, 4, "S")
         cp_x(0, 5, "S")
         m1(0, 6, "aux")
         m1(0, 7, "aux")
         qx(0, 1, 1)
-        cp_x(0, 6, "V")
+        m2(2)
+        cp_x(0, 6, "S")
         cp_x(0, 7, "S")
         tr(1, 0)
         tr(1, 1)
         mx(0)
-        m2(2)
         cp_t(1, 0, "S")
         cp_t(1, 1, "S")
         qn(1, 0, 2)

@@ -20,6 +20,7 @@ NT = B * RT
 NORM = 1.0 / math.sqrt(F)
 FLOPS = 2 * B * (N * F * F + N * N * F)
 
+GROUP = 2
 SINGLES = 2
 MANUAL = False
 NRM_G = False
@@ -34,10 +35,10 @@ def tile_scalarproductattentiont_pa_t_kernel(tc, nodes, W, out):
     with ExitStack() as ctx:
         keep = ctx.enter_context(tc.tile_pool(name="keep", bufs=1))
         grp = ctx.enter_context(tc.tile_pool(name="grp", bufs=2))
-        epool = ctx.enter_context(tc.tile_pool(name="epool", bufs=8))
+        epool = ctx.enter_context(tc.tile_pool(name="epool", bufs=12))
         small = ctx.enter_context(tc.tile_pool(name="small", bufs=8))
-        ps_pr = ctx.enter_context(tc.psum_pool(name="ps_pr", bufs=3))
-        ps_aux = ctx.enter_context(tc.psum_pool(name="ps_aux", bufs=2))
+        ps_pr = ctx.enter_context(tc.psum_pool(name="ps_pr", bufs=2))
+        ps_aux = ctx.enter_context(tc.psum_pool(name="ps_aux", bufs=4))
         if MANUAL:
             ctx.enter_context(tc.manual_schedule())
 
@@ -193,57 +194,43 @@ def tile_scalarproductattentiont_pa_t_kernel(tc, nodes, W, out):
                 banks.append(pt)
             pr[i] = banks
 
-        def mx(i):
-            if i >= NT:
-                return
-            nb = small.tile([P, 1], F32, name="nb", tag="nb")
-            if ACCUM_MAX:
-                na = small.tile([P, 1], F32, name="na", tag="na")
-                nc.vector.tensor_scalar(
-                    out=junk[:], in0=pr[i][0][:], scalar1=-NORM, scalar2=None,
-                    op0=ALU.mult, op1=ALU.min, accum_out=na[:],
-                )
-                nc.vector.tensor_scalar(
-                    out=junk[:], in0=pr[i][1][:], scalar1=-NORM, scalar2=na[:],
-                    op0=ALU.mult, op1=ALU.min, accum_out=nb[:],
-                )
-            else:
-                m = small.tile([P, 2], F32, name="m", tag="m")
-                for h in range(2):
-                    nc.vector.tensor_reduce(out=m[:, h : h + 1], in_=pr[i][h][:], axis=AX.X, op=ALU.max)
-                nc.vector.tensor_scalar(
-                    out=nb[:], in0=m[:, 0:1], scalar1=m[:, 1:2], scalar2=-NORM, op0=ALU.max, op1=ALU.mult
-                )
-            st[("nb", i)] = nb
-
         def group_of(i):
             if i >= NT - SINGLES:
                 return i, 1
-            return i - i % 2, 2
+            return i - i % GROUP, GROUP
+
+        def mx(i):
+            if i >= NT:
+                return
+            e = epool.tile([P, N], F32, name="e", tag="e")
+            na = small.tile([P, 1], F32, name="na", tag="na")
+            nb = small.tile([P, 1], F32, name="nb", tag="nb")
+            nc.vector.tensor_scalar(
+                out=e[:, 0:512], in0=pr[i][0][:], scalar1=-NORM, scalar2=None,
+                op0=ALU.mult, op1=ALU.min, accum_out=na[:],
+            )
+            nc.vector.tensor_scalar(
+                out=e[:, 512:1024], in0=pr[i][1][:], scalar1=-NORM, scalar2=na[:],
+                op0=ALU.mult, op1=ALU.min, accum_out=nb[:],
+            )
+            st[("nb", i)] = nb
+            st[("e", i)] = e
 
         def ex(i):
             g0, gn = group_of(i)
-            e = epool.tile([P, N], F32, name="e", tag="e")
+            e = st[("e", i)]
             if i == g0:
-                st[("ss", g0)] = small.tile([P, gn, 2], F32, name="ss", tag="ss")
+                st[("ss", g0)] = small.tile([P, gn], F32, name="ss", tag="ss")
             ss = st[("ss", g0)]
-            for h in range(2):
-                nc.scalar.activation(
-                    out=e[:, 512 * h : 512 * h + 512],
-                    in_=pr[i][h][:],
-                    func=ACT.Exp,
-                    bias=st[("nb", i)][:],
-                    scale=NORM,
-                    accum_out=ss[:, i - g0, h : h + 1],
-                )
-            st[("e", i)] = e
+            nc.scalar.activation(
+                out=e[:], in_=e[:], func=ACT.Exp, bias=st[("nb", i)][:], scale=-1.0,
+                accum_out=ss[:, i - g0 : i - g0 + 1],
+            )
 
         def sums(g0):
             gn = group_of(g0)[1]
-            tot = small.tile([P, gn], F32, name="tot", tag="tot")
-            nc.vector.tensor_reduce(out=tot[:], in_=st[("ss", g0)][:], axis=AX.X, op=ALU.add)
             rr = small.tile([P, gn], F32, name="rr", tag="rr")
-            nc.vector.reciprocal(out=rr[:], in_=tot[:])
+            nc.vector.reciprocal(out=rr[:], in_=st[("ss", g0)][:])
             st[("rr", g0)] = rr
 
         def nrm(i, s_from):
@@ -275,7 +262,7 @@ def tile_scalarproductattentiont_pa_t_kernel(tc, nodes, W, out):
 
         tr(0, 0, "aux")
         tr(0, 1, "aux")
-        tr(0, 2, "prA")
+        tr(0, 2, "aux")
         w_piece(0, "V")
         w_piece(1, "V")
         w_piece(2, "S")
@@ -284,9 +271,9 @@ def tile_scalarproductattentiont_pa_t_kernel(tc, nodes, W, out):
         cp_t(0, 0, "S")
         qn(0, 0, 1)
         cp_t(0, 1, "S")
-        m1(0, 0, "prB")
-        m1(0, 1, "prA")
-        tr(0, 3, "prB")
+        m1(0, 0, "prA")
+        m1(0, 1, "prB")
+        tr(0, 3, "aux")
         qn(0, 1, 1)
         cp_t(0, 2, "S")
         cp_x(0, 0, "S")
@@ -308,12 +295,12 @@ def tile_scalarproductattentiont_pa_t_kernel(tc, nodes, W, out):
         m1(0, 6, "aux")
         m1(0, 7, "aux")
         qx(0, 1, 1)
-        m2(2)
         cp_x(0, 6, "S")
         cp_x(0, 7, "S")
         tr(1, 0)
         tr(1, 1)
         mx(0)
+        m2(2)
         cp_t(1, 0, "S")
         cp_t(1, 1, "S")
         qn(1, 0, 2)

from contextlib import ExitStack
import math

import concourse.mybir as mybir
from concourse.masks import make_identity

F32 = mybir.dt.float32
BF16 = mybir.dt.bfloat16
U32 = mybir.dt.uint32
U8 = mybir.dt.uint8
FP8X4 = mybir.dt.float8_e4m3fn_x4
ALU = mybir.AluOpType
ACT = mybir.ActivationFunctionType
AX = mybir.AxisListType

B, N, F = 4, 1024, 512
P = 128
RT = N // P
NT = B * RT
NORM = 1.0 / math.sqrt(F)
FLOPS = 2 * B * (N * F * F + N * N * F)

GROUP = 2
SINGLES = 2
MANUAL = False
NRM_G = False
ACCUM_MAX = False
S_FROM_LAST = 576
S_FROM = 1024
V_CPT = []


def tile_scalarproductattentiont_pa_t_kernel(tc, nodes, W, out):
    nc = tc.nc
    with ExitStack() as ctx:
        keep = ctx.enter_context(tc.tile_pool(name="keep", bufs=1))
        grp = ctx.enter_context(tc.tile_pool(name="grp", bufs=2))
        epool = ctx.enter_context(tc.tile_pool(name="epool", bufs=12))
        small = ctx.enter_context(tc.tile_pool(name="small", bufs=8))
        ps_pr = ctx.enter_context(tc.psum_pool(name="ps_pr", bufs=2))
        ps_aux = ctx.enter_context(tc.psum_pool(name="ps_aux", bufs=4))
        if MANUAL:
            ctx.enter_context(tc.manual_schedule())

        ident = keep.tile([P, P], F32, name="ident")
        make_identity(nc, ident[:])

        warm = keep.tile([P, 1], F32, name="warm")
        nc.vector.memset(warm[:], 0.0)
        nc.scalar.activation(out=warm[:], in_=warm[:], func=ACT.Exp)

        w_raw = keep.tile([P, 4, F], BF16, name="w_raw")
        nc.sync.dma_start(
            out=w_raw[:].rearrange("p (u e) c -> p u (e c)", u=2),
            in_=W.rearrange("(u q e) c -> q u (e c)", u=2, e=2),
        )
        nd = [keep.tile([P, RT, F], BF16, name="nd%d" % b) for b in range(B)]
        for j in range(4):
            nc.sync.dma_start(
                out=nd[0][:, 2 * j : 2 * j + 2, :],
                in_=nodes[0, 256 * j : 256 * j + 256, :].rearrange("(p r) f -> p r f", r=2),
            )
        for b in range(1, B):
            nc.sync.dma_start(
                out=nd[b][:].rearrange("p (j r) f -> p j (r f)", r=2),
                in_=nodes[b].rearrange("(j p r) f -> p j (r f)", p=P, r=2),
            )

        w_grp = keep.tile([P, 4 * F], BF16, name="w_grp", align_bytes=64)
        w_cod = keep.tile([P, F], U32, name="w_cod", align_bytes=64)
        w_scl = keep.tile([P, F], U8, name="w_scl", align_bytes=64)
        junk = keep.tile([P, 512], F32, name="junk") if ACCUM_MAX else None

        n_grp = {}
        x_grp = {}
        n_cod = [keep.tile([P, N], U32, name="n_cod%d" % b, align_bytes=64) for b in range(B)]
        n_scl = [keep.tile([P, N], U8, name="n_scl%d" % b, align_bytes=64) for b in range(B)]
        x_cod = [keep.tile([P, N], U32, name="x_cod%d" % b, align_bytes=64) for b in range(B)]
        x_scl = [keep.tile([P, N], U8, name="x_scl%d" % b, align_bytes=64) for b in range(B)]
        aux = {}
        pr = {}
        st = {}

        def aux_tile(tag):
            if tag == "aux":
                return ps_aux.tile([P, 4, P], F32, name="aux", tag="aux")
            return ps_pr.tile([P, 4, P], F32, name=tag, tag=tag)

        def copy(eng, dst, srcv):
            if eng == "S":
                nc.scalar.copy(out=dst, in_=srcv)
            else:
                nc.vector.tensor_copy(out=dst, in_=srcv)

        def w_piece(t, eng):
            w_view = w_raw[:].rearrange("p t (u m e) -> p t u m e", u=2, e=2)
            copy(
                eng,
                w_grp[:, 512 * t : 512 * t + 512].rearrange("p (m t) -> p m t", t=4),
                w_view[:, :, t // 2, :, t % 2].rearrange("p t m -> p m t"),
            )

        def w_quant():
            nc.vector.quantize_mx(out=w_cod[:].bitcast(FP8X4), scales=w_scl[:], in_=w_grp[:])

        def tr(b, j, tag="aux"):
            if b >= B:
                return
            tp = aux_tile(tag)
            aux[("t", b, j)] = tp
            for r2 in range(2):
                words = nd[b][:, 2 * j + r2, :].bitcast(F32)
                for u in range(2):
                    nc.tensor.transpose(tp[:, 2 * r2 + u, :], words[:, P * u : P * u + P], ident[:])

        def cp_t(b, j, eng):
            if b >= B:
                return
            if j == 0:
                n_grp[b] = grp.tile([P, 4 * N], BF16, name="n_grp", tag="n_grp", align_bytes=64)
            tp = aux[("t", b, j)]
            dst = n_grp[b][:, 1024 * j : 1024 * j + 1024].bitcast(F32)
            copy(
                eng,
                dst.rearrange("p (n r u) -> p n r u", r=2, u=2),
                tp[:].rearrange("p (r u) n -> p n r u", r=2),
            )

        def quant(b, cod, scl, grouped, q0, nq):
            if b >= B:
                return
            cols = slice(256 * q0, 256 * (q0 + nq))
            nc.vector.quantize_mx(
                out=cod[b][:, cols].bitcast(FP8X4),
                scales=scl[b][:, cols],
                in_=grouped[b][:, 1024 * q0 : 1024 * (q0 + nq)],
            )

        def qn(b, q0, nq):
            quant(b, n_cod, n_scl, n_grp, q0, nq)

        def qx(b, q0, nq):
            quant(b, x_cod, x_scl, x_grp, q0, nq)

        def m1(b, c, tag="aux"):
            if b >= B:
                return
            px = aux_tile(tag)
            aux[("x", b, c)] = px
            cols = slice(P * c, P * c + P)
            for t in range(4):
                wc = slice(P * t, P * t + P)
                nc.tensor.matmul_mx(
                    out=px[:, t, :],
                    lhsT=w_cod[:, wc].bitcast(FP8X4),
                    lhsT_scale=w_scl[:, wc],
                    rhs=n_cod[b][:, cols].bitcast(FP8X4),
                    rhs_scale=n_scl[b][:, cols],
                    start=True,
                    stop=True,
                )

        def cp_x(b, c, eng):
            if b >= B:
                return
            if c == 0:
                x_grp[b] = grp.tile([P, 4 * N], BF16, name="x_grp", tag="x_grp", align_bytes=64)
            px = aux[("x", b, c)]
            copy(
                eng,
                x_grp[b][:, 512 * c : 512 * c + 512].rearrange("p (n t) -> p n t", t=4),
                px[:].rearrange("p t n -> p n t"),
            )

        def m2(i):
            if i >= NT:
                return
            b, r = divmod(i, RT)
            rows = slice(P * r, P * r + P)
            banks = []
            for h in range(2):
                tag = "prA" if h == 0 else "prB"
                pt = ps_pr.tile([P, 512], F32, name=tag, tag=tag)
                cols = slice(512 * h, 512 * h + 512)
                nc.tensor.matmul_mx(
                    out=pt[:],
                    lhsT=x_cod[b][:, rows].bitcast(FP8X4),
                    lhsT_scale=x_scl[b][:, rows],
                    rhs=n_cod[b][:, cols].bitcast(FP8X4),
                    rhs_scale=n_scl[b][:, cols],
                    start=True,
                    stop=True,
                )
                banks.append(pt)
            pr[i] = banks

        def group_of(i):
            if i >= NT - SINGLES:
                return i, 1
            return i - i % GROUP, GROUP

        def mx(i):
            if i >= NT:
                return
            e = epool.tile([P, N], F32, name="e", tag="e")
            na = small.tile([P, 1], F32, name="na", tag="na")
            nb = small.tile([P, 1], F32, name="nb", tag="nb")
            nc.vector.tensor_scalar(
                out=e[:, 0:512], in0=pr[i][0][:], scalar1=-NORM, scalar2=None,
                op0=ALU.mult, op1=ALU.min, accum_out=na[:],
            )
            nc.vector.tensor_scalar(
                out=e[:, 512:1024], in0=pr[i][1][:], scalar1=-NORM, scalar2=na[:],
                op0=ALU.mult, op1=ALU.min, accum_out=nb[:],
            )
            st[("nb", i)] = nb
            st[("e", i)] = e

        def ex(i):
            g0, gn = group_of(i)
            e = st[("e", i)]
            if i == g0:
                st[("ss", g0)] = small.tile([P, gn], F32, name="ss", tag="ss")
            ss = st[("ss", g0)]
            nc.scalar.activation(
                out=e[:], in_=e[:], func=ACT.Exp, bias=st[("nb", i)][:], scale=-1.0,
                accum_out=ss[:, i - g0 : i - g0 + 1],
            )

        def sums(g0):
            gn = group_of(g0)[1]
            rr = small.tile([P, gn], F32, name="rr", tag="rr")
            nc.vector.reciprocal(out=rr[:], in_=st[("ss", g0)][:])
            st[("rr", g0)] = rr

        def nrm(i, s_from):
            b, r = divmod(i, RT)
            g0 = group_of(i)[0]
            e = st[("e", i)]
            rr = st[("rr", g0)][:, i - g0 : i - g0 + 1]
            nc.vector.tensor_scalar(
                out=e[:, 0:s_from], in0=e[:, 0:s_from], scalar1=rr, scalar2=None, op0=ALU.mult
            )
            if s_from < N:
                nc.scalar.activation(out=e[:, s_from:N], in_=e[:, s_from:N], func=ACT.Copy, scale=rr)
            nc.sync.dma_start(out=out[b, P * r : P * r + P, :], in_=e[:])

        done = []

        def finish(upto, s_from, most):
            k = 0
            while len(done) <= upto and k < most:
                i = len(done)
                g0, gn = group_of(i)
                if g0 + gn - 1 > upto:
                    return
                if i == g0:
                    sums(g0)
                nrm(i, s_from)
                done.append(i)
                k += 1

        tr(0, 0, "aux")
        tr(0, 1, "aux")
        tr(0, 2, "aux")
        w_piece(0, "V")
        w_piece(1, "V")
        w_piece(2, "S")
        w_piece(3, "S")
        w_quant()
        cp_t(0, 0, "S")
        qn(0, 0, 1)
        cp_t(0, 1, "S")
        m1(0, 0, "prA")
        m1(0, 1, "prB")
        tr(0, 3, "aux")
        qn(0, 1, 1)
        cp_t(0, 2, "S")
        cp_x(0, 0, "S")
        cp_x(0, 1, "S")
        m1(0, 2, "prA")
        m1(0, 3, "prB")
        qn(0, 2, 1)
        cp_t(0, 3, "S")
        qx(0, 0, 1)
        qn(0, 3, 1)
        m2(0)
        m1(0, 4, "aux")
        m1(0, 5, "aux")
        cp_x(0, 2, "S")
        cp_x(0, 3, "S")
        m2(1)
        cp_x(0, 4, "S")
        cp_x(0, 5, "S")
        m1(0, 6, "aux")
        m1(0, 7, "aux")
        qx(0, 1, 1)
        cp_x(0, 6, "S")
        cp_x(0, 7, "S")
        tr(1, 0)
        tr(1, 1)
        mx(0)
        m2(2)
        cp_t(1, 0, "S")
        cp_t(1, 1, "S")
        qn(1, 0, 2)
        m1(1, 0)

        for s in range(NT):
            b, r = divmod(s, RT)
            nx = b + 1
            mx(s + 1)
            finish(s - 1, S_FROM_LAST if s >= NT - RT else S_FROM, 2 if s >= NT - 2 else 1)
            ex(s)
            m2(s + 3)
            if r == 0:
                qx(b, 2, 2)
            elif r == 3:
                qn(nx, 2, 2)
            elif r == 4:
                qx(nx, 0, 2)
            elif r == 7:
                qn(nx + 1, 0, 2)
            cp_x(nx, r, "S")
            eng = "V" if r in V_CPT else "S"
            if r == 1:
                cp_t(nx, 2, eng)
            elif r == 2:
                cp_t(nx, 3, eng)
            elif r == 5:
                cp_t(nx + 1, 0, eng)
            elif r == 6:
                cp_t(nx + 1, 1, eng)
            if r < RT - 1:
                m1(nx, r + 1)
            else:
                m1(nx + 1, 0)
            if r == 0:
                tr(nx, 2)
            elif r == 1:
                tr(nx, 3)
            elif r == 4:
                tr(nx + 1, 0)
            elif r == 5:
                tr(nx + 1, 1)
        finish(NT - 1, S_FROM_LAST, NT)
